import numpy as np
import ml_dtypes


def mxq(x, axis, fmt="e4m3"):
    dtype, down = {"e4m3": (ml_dtypes.float8_e4m3fn, 7), "e5m2": (ml_dtypes.float8_e5m2, 14)}[fmt]
    v = np.moveaxis(np.asarray(x, np.float32).astype(ml_dtypes.bfloat16).astype(np.float64), axis, -1)
    blocks = v.reshape(v.shape[:-1] + (-1, 32))
    amax = np.abs(blocks).max(-1, keepdims=True)
    byte = np.maximum(np.where(amax > 0, np.frexp(amax)[1] - 1 + 127, 0) - down, 1)
    scale = np.exp2(byte - 127.0)
    codes = (blocks / scale).astype(np.float32).astype(dtype).astype(np.float64)
    return np.moveaxis((codes * scale).reshape(v.shape), -1, axis)


WIDE = False


def mx_kscale(k):
    if not WIDE:
        return np.ones(k)
    levels = np.array([20, -20, 10, -10, 0])
    a = np.random.permutation(np.resize(levels, k // 512 * 4)).reshape(k // 512, 4)
    idx = np.arange(k)
    return np.exp2(a[idx // 512, idx % 128 // 32])


BF16 = ml_dtypes.bfloat16


def bf(x):
    return np.asarray(x, np.float32).astype(BF16)


def f64(x):
    return np.asarray(x).astype(np.float64)


BATCH, V_NODES, DEG = 512, 512, 4
EDGES = V_NODES * DEG


def _build_masks():
    v_of_edge = np.repeat(np.arange(V_NODES), DEG)
    input_mask = (np.arange(V_NODES)[:, None] == v_of_edge[None, :]).astype(np.float64)
    same_v = v_of_edge[:, None] == v_of_edge[None, :]
    prev_mask = (same_v & ~np.eye(EDGES, dtype=bool)).astype(np.float64)
    return input_mask, prev_mask


def setup_inputs():
    u = mx_kscale(EDGES)
    input_mask, prev_mask = _build_masks()
    input_mask = input_mask + 0.02 * np.random.standard_normal((V_NODES, EDGES))
    prev_mask = prev_mask + 0.02 * np.random.standard_normal((EDGES, EDGES))
    x_in = np.random.standard_normal((BATCH, V_NODES))
    x_prev = np.random.standard_normal((BATCH, EDGES))
    g = np.random.standard_normal((BATCH, EDGES)) * np.exp2(np.random.randint(-12, 1, (BATCH, 1))) * 4.0 * u
    return {"x_in": bf(x_in),
            "x_prev": bf(x_prev),
            "input_mask": bf(input_mask / u[None, :]),
            "prev_mask": bf(prev_mask / u[None, :]),
            "grad_out": bf(g)}


def reference(x_in, x_prev, input_mask, prev_mask, grad_out):
    return mxq(f64(grad_out), 1, "e5m2") @ mxq(f64(prev_mask), 1, "e4m3").T

@@ -1,0 +1,122 @@
+from contextlib import ExitStack
+
+import concourse.mybir as mybir
+from concourse.masks import make_identity
+
+F32 = mybir.dt.float32
+BF16 = mybir.dt.bfloat16
+U32 = mybir.dt.uint32
+U8 = mybir.dt.uint8
+E4M3 = mybir.dt.float8_e4m3fn_x4
+E5M2 = mybir.dt.float8_e5m2_x4
+
+P = 128
+BATCH = 512
+EDGES = 2048
+K = 2048
+K_PASS = 512
+PASSES = K // K_PASS
+CHUNK = 512
+BLOCKS = CHUNK // P
+N_CHUNKS = EDGES // CHUNK
+
+FLOPS = 2 * BATCH * EDGES * K
+BYTES = 2 * (EDGES * K + BATCH * K) + 4 * BATCH * EDGES
+
+
+def tile_oddlayer_kernel(tc, x_in, x_prev, input_mask, prev_mask, grad_out, out):
+    nc = tc.nc
+    with ExitStack() as ctx:
+        ctx.enter_context(tc.manual_schedule())
+        const = ctx.enter_context(tc.tile_pool(name="const", bufs=1))
+        raw_pool = ctx.enter_context(tc.tile_pool(name="raw", bufs=1))
+        grp_pool = ctx.enter_context(tc.tile_pool(name="grp", bufs=3))
+        mx_pool = ctx.enter_context(tc.tile_pool(name="mx", bufs=1))
+        out_pool = ctx.enter_context(tc.tile_pool(name="outs", bufs=8))
+        psum_t = ctx.enter_context(tc.psum_pool(name="psum_t", bufs=6))
+        psum_a = ctx.enter_context(tc.psum_pool(name="psum_a", bufs=2))
+
+        sources = [grad_out] + [prev_mask[j * CHUNK:(j + 1) * CHUNK, :] for j in range(N_CHUNKS)]
+        raw = []
+        for s, src in enumerate(sources):
+            tiles = []
+            for r in range(BLOCKS):
+                t = raw_pool.tile([P, K], BF16, name="raw_%d_%d" % (s, r))
+                nc.sync.dma_start(out=t[:], in_=src[r * P:(r + 1) * P, :])
+                tiles.append(t)
+            raw.append(tiles)
+
+        ident = const.tile([P, P], F32, name="ident")
+        make_identity(nc, ident[:])
+
+        codes = []
+        scales = []
+        for s in range(len(sources)):
+            codes.append(mx_pool.tile([P, PASSES * CHUNK], U32, name="codes_%d" % s, align_bytes=64))
+            scales.append(mx_pool.tile([P, PASSES * CHUNK], U8, name="scales_%d" % s, align_bytes=64))
+
+        grouped = {}
+
+        def transposes(s):
+            g = grp_pool.tile([P, PASSES * CHUNK * 4], BF16, name="grouped", align_bytes=64)
+            grouped[s] = g
+            gw = g[:].bitcast(F32).rearrange("p (c e u) -> p c e u", c=PASSES, u=2)
+            for r in range(BLOCKS):
+                words = raw[s][r][:].bitcast(F32)
+                for h in range(2):
+                    xt = psum_t.tile([P, 4, P], F32, name="xt")
+                    for cu in range(4):
+                        w0 = (4 * h + cu) * P
+                        nc.tensor.transpose(xt[:, cu, :], words[:, w0:w0 + P], ident[:])
+                    dst = gw[:, 2 * h:2 * h + 2, r * P:(r + 1) * P, :]
+                    src = xt[:].rearrange("p (c u) e -> p c e u", u=2)
+                    if h == 0:
+                        nc.vector.tensor_copy(out=dst, in_=src)
+                    else:
+                        nc.scalar.copy(out=dst, in_=src)
+
+        def quantise(s):
+            fmt = E5M2 if s == 0 else E4M3
+            g = grouped[s]
+            half = PASSES * CHUNK // 2
+            for h in (1, 0):
+                nc.vector.quantize_mx(
+                    out=codes[s][:, h * half:(h + 1) * half].bitcast(fmt),
+                    scales=scales[s][:, h * half:(h + 1) * half],
+                    in_=g[:, h * half * 4:(h + 1) * half * 4],
+                )
+
+        def products(s, b_tiles):
+            j = s - 1
+            for bt in b_tiles:
+                acc = psum_a.tile([P, CHUNK], F32, name="acc")
+                for c in range(PASSES):
+                    m0 = c * CHUNK + bt * P
+                    nc.tensor.matmul_mx(
+                        out=acc[:],
+                        lhsT=codes[0][:, m0:m0 + P].bitcast(E5M2),
+                        lhsT_scale=scales[0][:, m0:m0 + P],
+                        rhs=codes[s][:, c * CHUNK:(c + 1) * CHUNK].bitcast(E4M3),
+                        rhs_scale=scales[s][:, c * CHUNK:(c + 1) * CHUNK],
+                        start=(c == 0),
+                        stop=(c == PASSES - 1),
+                    )
+                res = out_pool.tile([P, CHUNK], F32, name="res")
+                nc.scalar.copy(out=res[:], in_=acc[:])
+                nc.sync.dma_start(out=out[bt * P:(bt + 1) * P, j * CHUNK:(j + 1) * CHUNK], in_=res[:])
+
+        transposes(0)
+        quantise(0)
+        transposes(1)
+        quantise(1)
+        products(1, (0, 1))
+        transposes(2)
+        quantise(2)
+        products(1, (2, 3))
+        transposes(3)
+        quantise(3)
+        products(2, (0, 1, 2, 3))
+        transposes(4)
+        quantise(4)
+        products(3, (0, 1, 2, 3))
+        products(4, (0, 1, 2, 3))

@@ -19,6 +19,7 @@ PASSES = K // K_PASS
 CHUNK = 512
 BLOCKS = CHUNK // P
 N_CHUNKS = EDGES // CHUNK
+B_TILES = BATCH // P
 
 FLOPS = 2 * BATCH * EDGES * K
 BYTES = 2 * (EDGES * K + BATCH * K) + 4 * BATCH * EDGES
@@ -30,93 +31,132 @@ def tile_oddlayer_kernel(tc, x_in, x_prev, input_mask, prev_mask, grad_out, out)
         ctx.enter_context(tc.manual_schedule())
         const = ctx.enter_context(tc.tile_pool(name="const", bufs=1))
         raw_pool = ctx.enter_context(tc.tile_pool(name="raw", bufs=1))
-        grp_pool = ctx.enter_context(tc.tile_pool(name="grp", bufs=3))
+        grp_pool = ctx.enter_context(tc.tile_pool(name="grp", bufs=1))
+        grp3_pool = ctx.enter_context(tc.tile_pool(name="grp3", bufs=3))
         mx_pool = ctx.enter_context(tc.tile_pool(name="mx", bufs=1))
         out_pool = ctx.enter_context(tc.tile_pool(name="outs", bufs=8))
         psum_t = ctx.enter_context(tc.psum_pool(name="psum_t", bufs=6))
         psum_a = ctx.enter_context(tc.psum_pool(name="psum_a", bufs=2))
 
-        sources = [grad_out] + [prev_mask[j * CHUNK:(j + 1) * CHUNK, :] for j in range(N_CHUNKS)]
-        raw = []
-        for s, src in enumerate(sources):
-            tiles = []
+        g_raw = {}
+        p_raw = {}
+
+        def load_g(bt):
+            t = raw_pool.tile([P, K], BF16, name="g_raw_%d" % bt)
+            nc.sync.dma_start(out=t[:], in_=grad_out[bt * P:(bt + 1) * P, :])
+            g_raw[bt] = t
+
+        def load_p(j, r):
+            t = raw_pool.tile([P, K], BF16, name="p_raw_%d_%d" % (j, r))
+            row = j * CHUNK + r * P
+            nc.sync.dma_start(out=t[:], in_=prev_mask[row:row + P, :])
+            p_raw[(j, r)] = t
+
+        load_g(0)
+        for r in range(BLOCKS):
+            load_p(0, r)
+        for bt in range(1, B_TILES):
+            load_g(bt)
+        for j in range(1, N_CHUNKS):
             for r in range(BLOCKS):
-                t = raw_pool.tile([P, K], BF16, name="raw_%d_%d" % (s, r))
-                nc.sync.dma_start(out=t[:], in_=src[r * P:(r + 1) * P, :])
-                tiles.append(t)
-            raw.append(tiles)
+                load_p(j, r)
 
         ident = const.tile([P, P], F32, name="ident")
         make_identity(nc, ident[:])
 
-        codes = []
-        scales = []
-        for s in range(len(sources)):
-            codes.append(mx_pool.tile([P, PASSES * CHUNK], U32, name="codes_%d" % s, align_bytes=64))
-            scales.append(mx_pool.tile([P, PASSES * CHUNK], U8, name="scales_%d" % s, align_bytes=64))
+        g_grp = [grp_pool.tile([P, PASSES * P * 4], BF16, name="g_grp_%d" % bt, align_bytes=64) for bt in range(B_TILES)]
+        g_codes = [mx_pool.tile([P, PASSES * P], U32, name="g_codes_%d" % bt, align_bytes=64) for bt in range(B_TILES)]
+        g_scales = [mx_pool.tile([P, PASSES * P], U8, name="g_scales_%d" % bt, align_bytes=64) for bt in range(B_TILES)]
+        p_grp = {}
+        p_codes = [mx_pool.tile([P, PASSES * CHUNK], U32, name="p_codes_%d" % j, align_bytes=64) for j in range(N_CHUNKS)]
+        p_scales = [mx_pool.tile([P, PASSES * CHUNK], U8, name="p_scales_%d" % j, align_bytes=64) for j in range(N_CHUNKS)]
 
-        grouped = {}
+        def bank(raw_tile, dst, h, eng):
+            words = raw_tile[:].bitcast(F32)
+            xt = psum_t.tile([P, 4, P], F32, name="xt")
+            for cu in range(4):
+                w0 = (4 * h + cu) * P
+                nc.tensor.transpose(xt[:, cu, :], words[:, w0:w0 + P], ident[:])
+            src = xt[:].rearrange("p (c u) e -> p c e u", u=2)
+            if eng == "V":
+                nc.vector.tensor_copy(out=dst, in_=src)
+            else:
+                nc.scalar.copy(out=dst, in_=src)
 
-        def transposes(s):
-            g = grp_pool.tile([P, PASSES * CHUNK * 4], BF16, name="grouped", align_bytes=64)
-            grouped[s] = g
-            gw = g[:].bitcast(F32).rearrange("p (c e u) -> p c e u", c=PASSES, u=2)
-            for r in range(BLOCKS):
-                words = raw[s][r][:].bitcast(F32)
-                for h in range(2):
-                    xt = psum_t.tile([P, 4, P], F32, name="xt")
-                    for cu in range(4):
-                        w0 = (4 * h + cu) * P
-                        nc.tensor.transpose(xt[:, cu, :], words[:, w0:w0 + P], ident[:])
-                    dst = gw[:, 2 * h:2 * h + 2, r * P:(r + 1) * P, :]
-                    src = xt[:].rearrange("p (c u) e -> p c e u", u=2)
-                    if h == 0:
-                        nc.vector.tensor_copy(out=dst, in_=src)
-                    else:
-                        nc.scalar.copy(out=dst, in_=src)
+        def t_g(bt, e0="V", e1="S"):
+            gw = g_grp[bt][:].bitcast(F32).rearrange("p (c e u) -> p c e u", c=PASSES, u=2)
+            for h, eng in ((0, e0), (1, e1)):
+                bank(g_raw[bt], gw[:, 2 * h:2 * h + 2, :, :], h, eng)
 
-        def quantise(s):
-            fmt = E5M2 if s == 0 else E4M3
-            g = grouped[s]
-            half = PASSES * CHUNK // 2
-            for h in (1, 0):
-                nc.vector.quantize_mx(
-                    out=codes[s][:, h * half:(h + 1) * half].bitcast(fmt),
-                    scales=scales[s][:, h * half:(h + 1) * half],
-                    in_=g[:, h * half * 4:(h + 1) * half * 4],
+        def q_g(bt):
+            nc.vector.quantize_mx(out=g_codes[bt][:].bitcast(E5M2), scales=g_scales[bt][:], in_=g_grp[bt][:])
+
+        def t_p(j, r, e0="V", e1="S"):
+            if r == 0:
+                p_grp[j] = grp3_pool.tile([P, PASSES * CHUNK * 4], BF16, name="p_grp", align_bytes=64)
+            gw = p_grp[j][:].bitcast(F32).rearrange("p (c e u) -> p c e u", c=PASSES, u=2)
+            for h, eng in ((0, e0), (1, e1)):
+                bank(p_raw[(j, r)], gw[:, 2 * h:2 * h + 2, r * P:(r + 1) * P, :], h, eng)
+
+        def q_p(j, first, width):
+            nc.vector.quantize_mx(
+                out=p_codes[j][:, first:first + width].bitcast(E4M3),
+                scales=p_scales[j][:, first:first + width],
+                in_=p_grp[j][:, 4 * first:4 * (first + width)],
+            )
+
+        def q_pb(j, r):
+            for c in range(PASSES):
+                q_p(j, c * CHUNK + r * P, P)
+
+        def q_pc(j):
+            for h in range(2):
+                q_p(j, h * 2 * CHUNK, 2 * CHUNK)
+
+        def m(j, bt):
+            acc = psum_a.tile([P, CHUNK], F32, name="acc")
+            for c in range(PASSES):
+                nc.tensor.matmul_mx(
+                    out=acc[:],
+                    lhsT=g_codes[bt][:, c * P:(c + 1) * P].bitcast(E5M2),
+                    lhsT_scale=g_scales[bt][:, c * P:(c + 1) * P],
+                    rhs=p_codes[j][:, c * CHUNK:(c + 1) * CHUNK].bitcast(E4M3),
+                    rhs_scale=p_scales[j][:, c * CHUNK:(c + 1) * CHUNK],
+                    start=(c == 0),
+                    stop=(c == PASSES - 1),
                 )
+            res = out_pool.tile([P, CHUNK], F32, name="res")
+            nc.scalar.copy(out=res[:], in_=acc[:])
+            nc.sync.dma_start(out=out[bt * P:(bt + 1) * P, j * CHUNK:(j + 1) * CHUNK], in_=res[:])
 
-        def products(s, b_tiles):
-            j = s - 1
-            for bt in b_tiles:
-                acc = psum_a.tile([P, CHUNK], F32, name="acc")
-                for c in range(PASSES):
-                    m0 = c * CHUNK + bt * P
-                    nc.tensor.matmul_mx(
-                        out=acc[:],
-                        lhsT=codes[0][:, m0:m0 + P].bitcast(E5M2),
-                        lhsT_scale=scales[0][:, m0:m0 + P],
-                        rhs=codes[s][:, c * CHUNK:(c + 1) * CHUNK].bitcast(E4M3),
-                        rhs_scale=scales[s][:, c * CHUNK:(c + 1) * CHUNK],
-                        start=(c == 0),
-                        stop=(c == PASSES - 1),
-                    )
-                res = out_pool.tile([P, CHUNK], F32, name="res")
-                nc.scalar.copy(out=res[:], in_=acc[:])
-                nc.sync.dma_start(out=out[bt * P:(bt + 1) * P, j * CHUNK:(j + 1) * CHUNK], in_=res[:])
-
-        transposes(0)
-        quantise(0)
-        transposes(1)
-        quantise(1)
-        products(1, (0, 1))
-        transposes(2)
-        quantise(2)
-        products(1, (2, 3))
-        transposes(3)
-        quantise(3)
-        products(2, (0, 1, 2, 3))
-        transposes(4)
-        quantise(4)
-        products(3, (0, 1, 2, 3))
-        products(4, (0, 1, 2, 3))
+        t_g(0)
+        q_g(0)
+        t_p(0, 0, "S", "S")
+        q_pb(0, 0)
+        t_p(0, 1)
+        q_pb(0, 1)
+        t_p(0, 2, "S", "S")
+        q_pb(0, 2)
+        t_p(0, 3)
+        q_pb(0, 3)
+        t_g(1)
+        q_g(1)
+        m(0, 0)
+        t_g(2)
+        q_g(2)
+        m(0, 1)
+        t_g(3)
+        q_g(3)
+        for r in range(BLOCKS):
+            t_p(1, r)
+        m(0, 2)
+        q_pc(1)
+        m(0, 3)
+        for j in (1, 2):
+            for r in range(BLOCKS):
+                t_p(j + 1, r)
+            q_pc(j + 1)
+            for bt in range(B_TILES):
+                m(j, bt)
+        for bt in range(B_TILES):
+            m(3, bt)

@@ -35,8 +35,7 @@ def tile_oddlayer_kernel(tc, x_in, x_prev, input_mask, prev_mask, grad_out, out)
         grp3_pool = ctx.enter_context(tc.tile_pool(name="grp3", bufs=3))
         mx_pool = ctx.enter_context(tc.tile_pool(name="mx", bufs=1))
         out_pool = ctx.enter_context(tc.tile_pool(name="outs", bufs=8))
-        psum_t = ctx.enter_context(tc.psum_pool(name="psum_t", bufs=6))
-        psum_a = ctx.enter_context(tc.psum_pool(name="psum_a", bufs=2))
+        psum = ctx.enter_context(tc.psum_pool(name="psum", bufs=8))
 
         g_raw = {}
         p_raw = {}
@@ -73,7 +72,7 @@ def tile_oddlayer_kernel(tc, x_in, x_prev, input_mask, prev_mask, grad_out, out)
 
         def bank(raw_tile, dst, h, eng):
             words = raw_tile[:].bitcast(F32)
-            xt = psum_t.tile([P, 4, P], F32, name="xt")
+            xt = psum.tile([P, 4, P], F32, name="xt", tag="bank")
             for cu in range(4):
                 w0 = (4 * h + cu) * P
                 nc.tensor.transpose(xt[:, cu, :], words[:, w0:w0 + P], ident[:])
@@ -114,7 +113,7 @@ def tile_oddlayer_kernel(tc, x_in, x_prev, input_mask, prev_mask, grad_out, out)
                 q_p(j, h * 2 * CHUNK, 2 * CHUNK)
 
         def m(j, bt):
-            acc = psum_a.tile([P, CHUNK], F32, name="acc")
+            acc = psum.tile([P, CHUNK], F32, name="acc", tag="bank")
             for c in range(PASSES):
                 nc.tensor.matmul_mx(
                     out=acc[:],
@@ -125,9 +124,19 @@ def tile_oddlayer_kernel(tc, x_in, x_prev, input_mask, prev_mask, grad_out, out)
                     start=(c == 0),
                     stop=(c == PASSES - 1),
                 )
-            res = out_pool.tile([P, CHUNK], F32, name="res")
-            nc.scalar.copy(out=res[:], in_=acc[:])
-            nc.sync.dma_start(out=out[bt * P:(bt + 1) * P, j * CHUNK:(j + 1) * CHUNK], in_=res[:])
+            rows = out[bt * P:(bt + 1) * P, j * CHUNK:(j + 1) * CHUNK]
+            if j == N_CHUNKS - 1 and bt == B_TILES - 1:
+                half = CHUNK // 2
+                res_a = const.tile([P, half], F32, name="res_a")
+                res_b = const.tile([P, half], F32, name="res_b")
+                nc.vector.tensor_copy(out=res_a[:], in_=acc[:, 0:half])
+                nc.scalar.copy(out=res_b[:], in_=acc[:, half:CHUNK])
+                nc.sync.dma_start(out=rows[:, 0:half], in_=res_a[:])
+                nc.sync.dma_start(out=rows[:, half:CHUNK], in_=res_b[:])
+            else:
+                res = out_pool.tile([P, CHUNK], F32, name="res")
+                nc.scalar.copy(out=res[:], in_=acc[:])
+                nc.sync.dma_start(out=rows, in_=res[:])
 
         t_g(0)
         q_g(0)

@@ -60,6 +60,14 @@ def tile_oddlayer_kernel(tc, x_in, x_prev, input_mask, prev_mask, grad_out, out)
             for r in range(BLOCKS):
                 load_p(j, r)
 
+        warm = const.tile([P, CHUNK], BF16, name="warm")
+        nc.vector.memset(warm[:], 0.0)
+
+        def dummy(n):
+            d = psum.tile([P, CHUNK], F32, name="dummy", tag="bank")
+            for i in range(n):
+                nc.tensor.matmul(d[:], lhsT=warm[:, 0:P], rhs=warm[:], start=True, stop=True)
+
         ident = const.tile([P, P], F32, name="ident")
         make_identity(nc, ident[:])
 
@@ -138,18 +146,24 @@ def tile_oddlayer_kernel(tc, x_in, x_prev, input_mask, prev_mask, grad_out, out)
                 nc.scalar.copy(out=res[:], in_=acc[:])
                 nc.sync.dma_start(out=rows, in_=res[:])
 
+        dummy(6)
         t_g(0)
         q_g(0)
+        dummy(1)
         t_p(0, 0, "S", "S")
         q_pb(0, 0)
+        dummy(1)
         t_p(0, 1)
         q_pb(0, 1)
+        dummy(1)
         t_p(0, 2, "S", "S")
         q_pb(0, 2)
+        dummy(1)
         t_p(0, 3)
         q_pb(0, 3)
         t_g(1)
         q_g(1)
+        dummy(2)
         m(0, 0)
         t_g(2)
         q_g(2)

@@ -21,6 +21,9 @@ BLOCKS = CHUNK // P
 N_CHUNKS = EDGES // CHUNK
 B_TILES = BATCH // P
 
+PAD = 48
+SLOT = 256
+
 FLOPS = 2 * BATCH * EDGES * K
 BYTES = 2 * (EDGES * K + BATCH * K) + 4 * BATCH * EDGES
 
@@ -72,11 +75,11 @@ def tile_oddlayer_kernel(tc, x_in, x_prev, input_mask, prev_mask, grad_out, out)
         make_identity(nc, ident[:])
 
         g_grp = [grp_pool.tile([P, PASSES * P * 4], BF16, name="g_grp_%d" % bt, align_bytes=64) for bt in range(B_TILES)]
-        g_codes = [mx_pool.tile([P, PASSES * P], U32, name="g_codes_%d" % bt, align_bytes=64) for bt in range(B_TILES)]
-        g_scales = [mx_pool.tile([P, PASSES * P], U8, name="g_scales_%d" % bt, align_bytes=64) for bt in range(B_TILES)]
+        g_codes = [mx_pool.tile([P, PAD + PASSES * P], U32, name="g_codes_%d" % bt, align_bytes=256) for bt in range(B_TILES)]
+        g_scales = [mx_pool.tile([P, PASSES * SLOT], U8, name="g_scales_%d" % bt, align_bytes=256) for bt in range(B_TILES)]
         p_grp = {}
-        p_codes = [mx_pool.tile([P, PASSES * CHUNK], U32, name="p_codes_%d" % j, align_bytes=64) for j in range(N_CHUNKS)]
-        p_scales = [mx_pool.tile([P, PASSES * CHUNK], U8, name="p_scales_%d" % j, align_bytes=64) for j in range(N_CHUNKS)]
+        p_codes = [mx_pool.tile([P, PASSES * CHUNK], U32, name="p_codes_%d" % j, align_bytes=256) for j in range(N_CHUNKS)]
+        p_scales = [mx_pool.tile([P, PASSES * CHUNK], U8, name="p_scales_%d" % j, align_bytes=256) for j in range(N_CHUNKS)]
 
         def bank(raw_tile, dst, h, eng):
             words = raw_tile[:].bitcast(F32)
@@ -96,7 +99,12 @@ def tile_oddlayer_kernel(tc, x_in, x_prev, input_mask, prev_mask, grad_out, out)
                 bank(g_raw[bt], gw[:, 2 * h:2 * h + 2, :, :], h, eng)
 
         def q_g(bt):
-            nc.vector.quantize_mx(out=g_codes[bt][:].bitcast(E5M2), scales=g_scales[bt][:], in_=g_grp[bt][:])
+            for c in range(PASSES):
+                nc.vector.quantize_mx(
+                    out=g_codes[bt][:, PAD + c * P:PAD + (c + 1) * P].bitcast(E5M2),
+                    scales=g_scales[bt][:, c * SLOT:c * SLOT + P],
+                    in_=g_grp[bt][:, c * P * 4:(c + 1) * P * 4],
+                )
 
         def t_p(j, r, e0="V", e1="S"):
             if r == 0:
@@ -125,8 +133,8 @@ def tile_oddlayer_kernel(tc, x_in, x_prev, input_mask, prev_mask, grad_out, out)
             for c in range(PASSES):
                 nc.tensor.matmul_mx(
                     out=acc[:],
-                    lhsT=g_codes[bt][:, c * P:(c + 1) * P].bitcast(E5M2),
-                    lhsT_scale=g_scales[bt][:, c * P:(c + 1) * P],
+                    lhsT=g_codes[bt][:, PAD + c * P:PAD + (c + 1) * P].bitcast(E5M2),
+                    lhsT_scale=g_scales[bt][:, c * SLOT:c * SLOT + P],
                     rhs=p_codes[j][:, c * CHUNK:(c + 1) * CHUNK].bitcast(E4M3),
                     rhs_scale=p_scales[j][:, c * CHUNK:(c + 1) * CHUNK],
                     start=(c == 0),

from contextlib import ExitStack

import concourse.mybir as mybir
from concourse.masks import make_identity

F32 = mybir.dt.float32
BF16 = mybir.dt.bfloat16
U32 = mybir.dt.uint32
U8 = mybir.dt.uint8
E4M3 = mybir.dt.float8_e4m3fn_x4
E5M2 = mybir.dt.float8_e5m2_x4

P = 128
BATCH = 512
EDGES = 2048
K = 2048
K_PASS = 512
PASSES = K // K_PASS
CHUNK = 512
BLOCKS = CHUNK // P
N_CHUNKS = EDGES // CHUNK
B_TILES = BATCH // P

PAD = 48
SLOT = 256

FLOPS = 2 * BATCH * EDGES * K
BYTES = 2 * (EDGES * K + BATCH * K) + 4 * BATCH * EDGES


def tile_oddlayer_kernel(tc, x_in, x_prev, input_mask, prev_mask, grad_out, out):
    nc = tc.nc
    with ExitStack() as ctx:
        ctx.enter_context(tc.manual_schedule())
        const = ctx.enter_context(tc.tile_pool(name="const", bufs=1))
        raw_pool = ctx.enter_context(tc.tile_pool(name="raw", bufs=1))
        grp_pool = ctx.enter_context(tc.tile_pool(name="grp", bufs=1))
        grp3_pool = ctx.enter_context(tc.tile_pool(name="grp3", bufs=3))
        mx_pool = ctx.enter_context(tc.tile_pool(name="mx", bufs=1))
        out_pool = ctx.enter_context(tc.tile_pool(name="outs", bufs=8))
        psum = ctx.enter_context(tc.psum_pool(name="psum", bufs=8))

        g_raw = {}
        p_raw = {}

        def load_g(bt):
            t = raw_pool.tile([P, K], BF16, name="g_raw_%d" % bt)
            nc.sync.dma_start(out=t[:], in_=grad_out[bt * P:(bt + 1) * P, :])
            g_raw[bt] = t

        def load_p(j, r):
            t = raw_pool.tile([P, K], BF16, name="p_raw_%d_%d" % (j, r))
            row = j * CHUNK + r * P
            nc.sync.dma_start(out=t[:], in_=prev_mask[row:row + P, :])
            p_raw[(j, r)] = t

        load_g(0)
        for r in range(BLOCKS):
            load_p(0, r)
        for bt in range(1, B_TILES):
            load_g(bt)
        for j in range(1, N_CHUNKS):
            for r in range(BLOCKS):
                load_p(j, r)

        warm = const.tile([P, CHUNK], BF16, name="warm")
        nc.vector.memset(warm[:], 0.0)

        def dummy(n):
            d = psum.tile([P, CHUNK], F32, name="dummy", tag="bank")
            for i in range(n):
                nc.tensor.matmul(d[:], lhsT=warm[:, 0:P], rhs=warm[:], start=True, stop=True)

        ident = const.tile([P, P], F32, name="ident")
        make_identity(nc, ident[:])

        g_grp = [grp_pool.tile([P, PASSES * P * 4], BF16, name="g_grp_%d" % bt, align_bytes=64) for bt in range(B_TILES)]
        g_codes = [mx_pool.tile([P, PAD + PASSES * P], U32, name="g_codes_%d" % bt, align_bytes=256) for bt in range(B_TILES)]
        g_scales = [mx_pool.tile([P, PASSES * SLOT], U8, name="g_scales_%d" % bt, align_bytes=256) for bt in range(B_TILES)]
        p_grp = {}
        p_codes = [mx_pool.tile([P, PASSES * CHUNK], U32, name="p_codes_%d" % j, align_bytes=256) for j in range(N_CHUNKS)]
        p_scales = [mx_pool.tile([P, PASSES * CHUNK], U8, name="p_scales_%d" % j, align_bytes=256) for j in range(N_CHUNKS)]

        def bank(raw_tile, dst, h, eng):
            words = raw_tile[:].bitcast(F32)
            xt = psum.tile([P, 4, P], F32, name="xt", tag="bank")
            for cu in range(4):
                w0 = (4 * h + cu) * P
                nc.tensor.transpose(xt[:, cu, :], words[:, w0:w0 + P], ident[:])
            src = xt[:].rearrange("p (c u) e -> p c e u", u=2)
            if eng == "V":
                nc.vector.tensor_copy(out=dst, in_=src)
            else:
                nc.scalar.copy(out=dst, in_=src)

        def t_g(bt, e0="V", e1="S"):
            gw = g_grp[bt][:].bitcast(F32).rearrange("p (c e u) -> p c e u", c=PASSES, u=2)
            for h, eng in ((0, e0), (1, e1)):
                bank(g_raw[bt], gw[:, 2 * h:2 * h + 2, :, :], h, eng)

        def q_g(bt):
            for c in range(PASSES):
                nc.vector.quantize_mx(
                    out=g_codes[bt][:, PAD + c * P:PAD + (c + 1) * P].bitcast(E5M2),
                    scales=g_scales[bt][:, c * SLOT:c * SLOT + P],
                    in_=g_grp[bt][:, c * P * 4:(c + 1) * P * 4],
                )

        def t_p(j, r, e0="V", e1="S"):
            if r == 0:
                p_grp[j] = grp3_pool.tile([P, PASSES * CHUNK * 4], BF16, name="p_grp", align_bytes=64)
            gw = p_grp[j][:].bitcast(F32).rearrange("p (c e u) -> p c e u", c=PASSES, u=2)
            for h, eng in ((0, e0), (1, e1)):
                bank(p_raw[(j, r)], gw[:, 2 * h:2 * h + 2, r * P:(r + 1) * P, :], h, eng)

        def q_p(j, first, width):
            nc.vector.quantize_mx(
                out=p_codes[j][:, first:first + width].bitcast(E4M3),
                scales=p_scales[j][:, first:first + width],
                in_=p_grp[j][:, 4 * first:4 * (first + width)],
            )

        def q_pb(j, r):
            for c in range(PASSES):
                q_p(j, c * CHUNK + r * P, P)

        def q_pc(j):
            for h in range(2):
                q_p(j, h * 2 * CHUNK, 2 * CHUNK)

        def m(j, bt):
            acc = psum.tile([P, CHUNK], F32, name="acc", tag="bank")
            for c in range(PASSES):
                nc.tensor.matmul_mx(
                    out=acc[:],
                    lhsT=g_codes[bt][:, PAD + c * P:PAD + (c + 1) * P].bitcast(E5M2),
                    lhsT_scale=g_scales[bt][:, c * SLOT:c * SLOT + P],
                    rhs=p_codes[j][:, c * CHUNK:(c + 1) * CHUNK].bitcast(E4M3),
                    rhs_scale=p_scales[j][:, c * CHUNK:(c + 1) * CHUNK],
                    start=(c == 0),
                    stop=(c == PASSES - 1),
                )
            rows = out[bt * P:(bt + 1) * P, j * CHUNK:(j + 1) * CHUNK]
            if j == N_CHUNKS - 1 and bt == B_TILES - 1:
                half = CHUNK // 2
                res_a = const.tile([P, half], F32, name="res_a")
                res_b = const.tile([P, half], F32, name="res_b")
                nc.vector.tensor_copy(out=res_a[:], in_=acc[:, 0:half])
                nc.scalar.copy(out=res_b[:], in_=acc[:, half:CHUNK])
                nc.sync.dma_start(out=rows[:, 0:half], in_=res_a[:])
                nc.sync.dma_start(out=rows[:, half:CHUNK], in_=res_b[:])
            else:
                res = out_pool.tile([P, CHUNK], F32, name="res")
                nc.scalar.copy(out=res[:], in_=acc[:])
                nc.sync.dma_start(out=rows, in_=res[:])

        dummy(6)
        t_g(0)
        q_g(0)
        dummy(1)
        t_p(0, 0, "S", "S")
        q_pb(0, 0)
        dummy(1)
        t_p(0, 1)
        q_pb(0, 1)
        dummy(1)
        t_p(0, 2, "S", "S")
        q_pb(0, 2)
        dummy(1)
        t_p(0, 3)
        q_pb(0, 3)
        t_g(1)
        q_g(1)
        dummy(2)
        m(0, 0)
        t_g(2)
        q_g(2)
        m(0, 1)
        t_g(3)
        q_g(3)
        for r in range(BLOCKS):
            t_p(1, r)
        m(0, 2)
        q_pc(1)
        m(0, 3)
        for j in (1, 2):
            for r in range(BLOCKS):
                t_p(j + 1, r)
            q_pc(j + 1)
            for bt in range(B_TILES):
                m(j, bt)
        for bt in range(B_TILES):
            m(3, bt)
